import numpy as np
import ml_dtypes


def mxq(x, axis, fmt="e4m3"):
    dtype, down = {"e4m3": (ml_dtypes.float8_e4m3fn, 7), "e5m2": (ml_dtypes.float8_e5m2, 14)}[fmt]
    v = np.moveaxis(np.asarray(x, np.float32).astype(ml_dtypes.bfloat16).astype(np.float64), axis, -1)
    blocks = v.reshape(v.shape[:-1] + (-1, 32))
    amax = np.abs(blocks).max(-1, keepdims=True)
    byte = np.maximum(np.where(amax > 0, np.frexp(amax)[1] - 1 + 127, 0) - down, 1)
    scale = np.exp2(byte - 127.0)
    codes = (blocks / scale).astype(np.float32).astype(dtype).astype(np.float64)
    return np.moveaxis((codes * scale).reshape(v.shape), -1, axis)


WIDE = False


def mx_kscale(k):
    if not WIDE:
        return np.ones(k)
    levels = np.array([10, -10, 5, -5, 0])
    if k % 512:
        return np.exp2(np.random.permutation(np.resize(levels, k // 32))).repeat(32)
    a = np.empty((k // 512, 16))
    for p in range(k // 512):
        a[p, :8] = np.random.permutation(np.resize(levels, 8))
        for g in range(8):
            far = levels[np.abs(levels - a[p, g]) >= 10]
            a[p, g + 8] = far[np.random.randint(len(far))]
    return np.exp2(a.ravel()).repeat(32)


BF16 = ml_dtypes.bfloat16


def bf(x):
    return np.asarray(x, np.float32).astype(BF16)


def f64(x):
    return np.asarray(x).astype(np.float64)


E2M1 = np.array([0.0, 0.5, 1.0, 1.5, 2.0, 3.0, 4.0, 6.0, -0.0, -0.5, -1.0, -1.5, -2.0, -3.0, -4.0, -6.0])


def pack_weight(w, fmt):
    k, n = w.shape
    w = f64(bf(w)).reshape(k // 32, 32, n)
    amax = np.abs(w).max(1)
    if fmt == "e4m3":
        byte = np.frexp(amax)[1] - 1 + 127 - 7
    else:
        mant, ex = np.frexp(amax / 6.0)
        byte = np.where(mant > 0.5, ex, ex - 1) + 127
    byte = np.clip(np.where(amax > 0, byte, 1), 1, 254)
    scaled = (w * np.exp2(127.0 - byte)[:, None, :]).reshape(k, n).astype(np.float32)
    by_word = np.ascontiguousarray(scaled.reshape(k // 512, 128, 4, n).transpose(0, 1, 3, 2))
    if fmt == "e4m3":
        words = by_word.astype(ml_dtypes.float8_e4m3fn).view(np.uint8)
    else:
        c = by_word.astype(ml_dtypes.float4_e2m1fn).view(np.uint8) & 0xF
        words = c[..., 0::2] | (c[..., 1::2] << 4)
    return np.ascontiguousarray(words), np.ascontiguousarray(byte.astype(np.uint8).reshape(k // 512, 16, n))


def unpack_weight(words, scales, fmt):
    g, p, n, _ = words.shape
    if fmt == "e4m3":
        vals = np.ascontiguousarray(words).view(ml_dtypes.float8_e4m3fn).astype(np.float64)
    else:
        nib = np.empty((g, p, n, 4), np.uint8)
        nib[..., 0::2] = words & 0xF
        nib[..., 1::2] = words >> 4
        vals = E2M1[nib]
    vals = vals * np.repeat(np.exp2(scales.astype(np.float64) - 127.0), 8, axis=1)[..., None]
    return vals.transpose(0, 1, 3, 2).reshape(g * 512, n)
def pack4(w):
    words, scales = pack_weight(w, "e2m1")
    return words.reshape(words.shape[0], 128, -1), scales


def unpack4(words, scales):
    return unpack_weight(words.reshape(words.shape[0], 128, -1, 2), scales, "e2m1")


B, N, D, H, DH = 2, 512, 1024, 16, 64
INNER = H * DH
S = 2 * DH


def dpfp(u):
    u2 = np.concatenate([np.maximum(u, 0.0), np.maximum(-u, 0.0)], axis=-1)
    return u2 * np.roll(u2, 1, axis=-1)


def draw0():
    s, t = mx_kscale(D), mx_kscale(N)
    f = dpfp(np.random.standard_normal((B, H, N, DH)))
    x = bf(np.random.standard_normal((B, N, D)) * s)
    words, scales = pack4(np.random.standard_normal((D, INNER)) / np.sqrt(D) / s[:, None])
    return {"x": x,
            "wv_words": words,
            "wv_scales": scales,
            "beta": bf(np.random.standard_normal((B, H, N)) * t),
            "vo": bf(np.random.standard_normal((B, H, N, DH)) * 0.3),
            "k_phi": bf(f / f.sum(-1, keepdims=True) / t[:, None]),
            "W": bf(np.random.standard_normal((B, H, S, DH)))}


def core(x, wv_words, wv_scales, beta, vo, k_phi, W):
    v = mxq(f64(x), 2, "e4m3") @ unpack4(wv_words, wv_scales)
    v = v.reshape(B, N, H, DH).transpose(0, 2, 1, 3)
    dv = f64(beta)[..., None] * (v - f64(vo))
    return f64(W) + (mxq(f64(k_phi).transpose(0, 1, 3, 2), 3, "e4m3") @ mxq(dv, 2, "e4m3"))


def e4m3fn_bytes(y):
    return np.clip(np.asarray(y, np.float64), -448.0, 448.0).astype(np.float32).astype(ml_dtypes.float8_e4m3fn).view(np.uint8)


def e4m3fn_values(b):
    return np.asarray(b, np.uint8).view(ml_dtypes.float8_e4m3fn).astype(np.float64)


def setup_inputs():
    d = draw0()
    x0 = np.asarray(d['k_phi']).astype(np.float64)
    s = (np.max(np.abs(x0), axis=(0, 1, 3), keepdims=True) / 448.0).astype(np.float32)
    out = {}
    for k, v in d.items():
        if k == 'k_phi':
            out['k_phi_bytes'] = e4m3fn_bytes(x0 / s.astype(np.float64))
            out['k_phi_scale'] = s
        else:
            out[k] = v
    return out


def reference(x, wv_words, wv_scales, beta, vo, k_phi_bytes, k_phi_scale, W):
    return core(x, wv_words, wv_scales, beta, vo, e4m3fn_values(k_phi_bytes) * k_phi_scale.astype(np.float64), W)

@@ -1,0 +1,353 @@
+from contextlib import ExitStack
+
+import concourse.mybir as mybir
+from concourse.masks import make_identity
+
+F32 = mybir.dt.float32
+BF16 = mybir.dt.bfloat16
+I32 = mybir.dt.int32
+U32 = mybir.dt.uint32
+U8 = mybir.dt.uint8
+FP8 = mybir.dt.float8_e4m3fn
+E4M3X4 = mybir.dt.float8_e4m3fn_x4
+E2M1X4 = mybir.dt.float4_e2m1fn_x4
+ALU = mybir.AluOpType
+ACT = mybir.ActivationFunctionType
+
+B, N, D, H, DH = 2, 512, 1024, 16, 64
+S = 2 * DH
+P = 128
+PACK = 4
+FLOPS = 2 * B * N * D * H * DH + 2 * B * H * N * S * DH
+
+WIDEN_ON_VECTOR = ((0, 0), (0, 2), (0, 8), (0, 10))
+INTERLEAVE_ON_VECTOR = ((0, 0), (0, 2), (0, 8), (0, 10))
+
+
+def tile_dpfpattention_pb_w4_kernel(tc, x, wv_words, wv_scales, beta, vo, k_phi_bytes, k_phi_scale, W, out):
+    nc = tc.nc
+    with ExitStack() as ctx:
+        keep = ctx.enter_context(tc.tile_pool(name="keep", bufs=1))
+        work = ctx.enter_context(tc.tile_pool(name="work", bufs=4))
+        psum = ctx.enter_context(tc.psum_pool(name="psum", bufs=2))
+
+        warm = keep.tile([P, 1], F32, name="warm")
+        nc.gpsimd.memset(warm[:], 0.0)
+        nc.scalar.activation(out=warm[:], in_=warm[:], func=ACT.Copy)
+        ident = keep.tile([P, P], F32, name="ident")
+        make_identity(nc, ident[:])
+        wsc = keep.tile([P, 2, D], U8, align_bytes=64, name="wsc")
+        nc.gpsimd.memset(wsc[:].rearrange("p g n -> p (g n)").bitcast(I32), 0)
+        beta_rows = keep.tile([P, N], BF16, align_bytes=64, name="beta_rows")
+        nc.gpsimd.memset(beta_rows[:], 0.0)
+
+        kscale = keep.tile([P, PACK], F32, name="kscale")
+        nc.sync.dma_start(out=kscale[:], in_=k_phi_scale.rearrange("a c (p t) f -> p (a c t f)", t=PACK))
+        kb = {}
+
+        def load_kphi(b, h0, nh):
+            kbt = keep.tile([P, nh, PACK * S], U8, align_bytes=64, name=f"kb_{b}_{h0}")
+            nc.sync.dma_start(out=kbt[:], in_=k_phi_bytes[b, h0 : h0 + nh].rearrange("h (p t) s -> p h (t s)", t=PACK))
+            for h in range(nh):
+                kb[b, h0 + h] = kbt[:, h, :]
+
+        xs = {}
+
+        def load_x(b, t):
+            xt_ = keep.tile([P, D], BF16, align_bytes=64, name=f"x_{b}_{t}")
+            nc.sync.dma_start(out=xt_[:], in_=x[b].rearrange("(p t) k -> p t k", t=PACK)[:, t, :])
+            xs[b, t] = xt_
+
+        vos = {}
+
+        def load_vo(b, u):
+            v_ = keep.tile([P, 8, PACK, DH], BF16, align_bytes=64, name=f"vo_{b}_{u}")
+            nc.sync.dma_start(
+                out=v_[:].rearrange("p h t d -> p h (t d)"),
+                in_=vo[b, 8 * u : 8 * u + 8].rearrange("h (p t) d -> p h (t d)", t=PACK),
+            )
+            vos[b, u] = v_
+
+        ws = {}
+
+        def load_W(b):
+            w_ = keep.tile([P, H, DH], BF16, align_bytes=64, name=f"W_{b}")
+            nc.sync.dma_start(out=w_[:], in_=W[b].rearrange("h s d -> s h d"))
+            ws[b] = w_
+
+        load_kphi(0, 0, 2)
+        load_kphi(0, 4, 2)
+        load_kphi(0, 2, 2)
+        load_kphi(0, 8, 2)
+        for t in range(PACK):
+            load_x(0, t)
+        load_kphi(0, 10, 2)
+        load_kphi(0, 6, 2)
+        for q in range(4):
+            nc.sync.dma_start(
+                out=wsc[32 * q : 32 * q + 4, :, :].bitcast(I32),
+                in_=wv_scales[:, 4 * q : 4 * q + 4, :].rearrange("g q n -> q g n").bitcast(I32),
+            )
+        nc.sync.dma_start(out=beta_rows[0 : B * H, :], in_=beta.rearrange("b h n -> (b h) n"))
+        ww = keep.tile([P, 2, 2 * D], U8, align_bytes=64, name="ww")
+        nc.sync.dma_start(out=ww[:], in_=wv_words.rearrange("g p n -> p g n"))
+        load_vo(0, 0)
+        load_kphi(0, 12, 4)
+        load_vo(0, 1)
+        for t in range(PACK):
+            load_x(1, t)
+        load_kphi(1, 0, 8)
+        load_W(0)
+        load_vo(1, 0)
+        load_kphi(1, 8, 8)
+        load_vo(1, 1)
+        load_W(1)
+
+        beta_t = keep.tile([P, B * H, PACK], BF16, align_bytes=64, name="beta_t")
+
+        def make_beta():
+            bt = psum.tile([P, 2, P], F32, name="xt", bufs=2)
+            words = beta_rows[:].bitcast(F32)
+            for u in range(2):
+                nc.tensor.transpose(bt[:, u, :], words[:, u : 2 * P : 2], ident[:])
+            nc.vector.tensor_copy(
+                out=beta_t[:].rearrange("p r t -> p (r t)").bitcast(F32).rearrange("p (r u) -> p r u", u=2),
+                in_=bt[:, :, 0 : B * H].rearrange("p u r -> p r u"),
+            )
+
+        xg, xc = {}, {}
+
+        def turn_x(b, t):
+            ps = psum.tile([P, 2, 2, P], F32, name="xt", bufs=2)
+            words = xs[b, t][:].bitcast(F32)
+            for g in range(2):
+                for u in range(2):
+                    nc.tensor.transpose(ps[:, g, u, :], words[:, 256 * g + u : 256 * (g + 1) : 2], ident[:])
+            gt = work.tile([P, 2 * P * PACK], BF16, align_bytes=64, name="xg", bufs=4)
+            nc.scalar.copy(
+                out=gt[:].bitcast(F32).rearrange("p (g r u) -> p g r u", g=2, u=2),
+                in_=ps[:].rearrange("p g u r -> p g r u"),
+            )
+            xg[b, t] = gt
+
+        def quant_x(b, t):
+            codes = keep.tile([P, 2, P], U32, align_bytes=64, name=f"xc_{b}_{t}")
+            scales = keep.tile([P, 2, P], U8, align_bytes=64, name=f"xsc_{b}_{t}")
+            nc.vector.quantize_mx(
+                out=codes[:].rearrange("p g r -> p (g r)").bitcast(E4M3X4),
+                scales=scales[:].rearrange("p g r -> p (g r)"),
+                in_=xg[b, t][:],
+            )
+            xc[b, t] = (codes, scales)
+
+        planes, inter, kc = {}, {}, {}
+
+        def widen(b, h):
+            pl = work.tile([P, 2, PACK, S], BF16, align_bytes=64, name="planes", bufs=6)
+            for i in range(2):
+                for t in range(PACK):
+                    src = kb[b, h + i][:, S * t : S * (t + 1)].bitcast(FP8)
+                    if (b, h) in WIDEN_ON_VECTOR:
+                        nc.vector.tensor_scalar(out=pl[:, i, t, :], in0=src, scalar1=kscale[:, t : t + 1], scalar2=None, op0=ALU.mult)
+                    else:
+                        nc.scalar.activation(out=pl[:, i, t, :], in_=src, func=ACT.Copy, scale=kscale[:, t : t + 1])
+            planes[b, h] = pl
+
+        def interleave(b, h):
+            it = work.tile([P, 2, S, PACK], BF16, align_bytes=64, name="inter", bufs=6)
+            copy = nc.vector.tensor_copy if (b, h) in INTERLEAVE_ON_VECTOR else nc.scalar.copy
+            copy(out=it[:], in_=planes[b, h][:].rearrange("p h t s -> p h s t"))
+            inter[b, h] = it
+
+        def quant_k(b, h):
+            codes = keep.tile([P, 2, S], U32, align_bytes=64, name=f"kc_{b}_{h}")
+            scales = keep.tile([P, 2, S], U8, align_bytes=64, name=f"ksc_{b}_{h}")
+            nc.vector.quantize_mx(
+                out=codes[:].rearrange("p h s -> p (h s)").bitcast(E4M3X4),
+                scales=scales[:].rearrange("p h s -> p (h s)"),
+                in_=inter[b, h][:].rearrange("p h s t -> p (h s t)"),
+            )
+            for i in range(2):
+                kc[b, h + i] = (codes[:, i, :], scales[:, i, :])
+
+        vps, t1s, dvg, dvc = {}, {}, {}, {}
+
+        def values(b, u, t):
+            ps = psum.tile([P, 512], F32, name="v", bufs=4)
+            codes, scales = xc[b, t]
+            for g in range(2):
+                nc.tensor.matmul_mx(
+                    out=ps[:],
+                    lhsT=codes[:, g, :].bitcast(E4M3X4),
+                    lhsT_scale=scales[:, g, :],
+                    rhs=ww[:, g, 1024 * u : 1024 * (u + 1)].bitcast(E2M1X4),
+                    rhs_scale=wsc[:, g, 512 * u : 512 * (u + 1)],
+                    start=(g == 0),
+                    stop=(g == 1),
+                )
+            vps[b, u, t] = ps
+
+        def subtract(b, u, t):
+            if t == 0:
+                t1 = work.tile([P, PACK, 8, DH], F32, align_bytes=64, name="t1", bufs=2)
+                t1s[b, u] = t1
+            nc.vector.tensor_tensor(
+                out=t1s[b, u][:, t, :, :],
+                in0=vps[b, u, t][:].rearrange("p (h d) -> p h d", d=DH),
+                in1=vos[b, u][:, :, t, :],
+                op=ALU.subtract,
+            )
+
+        def scale_dv(b, u, i):
+            dg = work.tile([P, 4, DH, PACK], BF16, align_bytes=64, name="dvg", bufs=3)
+            r0 = 16 * b + 8 * u + 4 * i
+            nc.vector.tensor_tensor(
+                out=dg[:],
+                in0=t1s[b, u][:, :, 4 * i : 4 * i + 4, :].rearrange("p t h d -> p h d t"),
+                in1=beta_t[:, r0 : r0 + 4, :].unsqueeze(2).to_broadcast([P, 4, DH, PACK]),
+                op=ALU.mult,
+            )
+            dvg[b, u, i] = dg
+
+        def quant_dv(b, u, i):
+            codes = work.tile([P, 4, DH], U32, align_bytes=64, name="dvc", bufs=4)
+            scales = work.tile([P, 4, DH], U8, align_bytes=64, name="dvsc", bufs=4)
+            nc.vector.quantize_mx(
+                out=codes[:].rearrange("p h d -> p (h d)").bitcast(E4M3X4),
+                scales=scales[:].rearrange("p h d -> p (h d)"),
+                in_=dvg[b, u, i][:].rearrange("p h d t -> p (h d t)"),
+            )
+            dvc[b, u, i] = (codes, scales)
+
+        ops = {}
+
+        def update(b, u, i):
+            ps = psum.tile([P, 4, DH], F32, name="o", bufs=2)
+            dcodes, dscales = dvc[b, u, i]
+            for j in range(4):
+                kcodes, kscales = kc[b, 8 * u + 4 * i + j]
+                nc.tensor.matmul_mx(
+                    out=ps[:, j, :],
+                    lhsT=kcodes.bitcast(E4M3X4),
+                    lhsT_scale=kscales,
+                    rhs=dcodes[:, j, :].bitcast(E4M3X4),
+                    rhs_scale=dscales[:, j, :],
+                    start=True,
+                    stop=True,
+                )
+            ops[b, u, i] = ps
+
+        def finish(b, u, i):
+            h0 = 8 * u + 4 * i
+            ot = work.tile([P, 4, DH], F32, align_bytes=64, name="ot", bufs=4)
+            nc.vector.tensor_tensor(out=ot[:], in0=ops[b, u, i][:], in1=ws[b][:, h0 : h0 + 4, :], op=ALU.add)
+            nc.sync.dma_start(out=out[b, h0 : h0 + 4].rearrange("h s d -> s h d"), in_=ot[:])
+
+        def kphi(b, h):
+            widen(b, h)
+            interleave(b, h)
+            quant_k(b, h)
+
+
+        def body():
+            widen(0, 0)
+            widen(0, 4)
+            widen(0, 2)
+            interleave(0, 4)
+            interleave(0, 0)
+            widen(0, 8)
+            interleave(0, 2)
+            quant_k(0, 0)
+            turn_x(0, 0)
+            turn_x(0, 1)
+            widen(0, 6)
+            widen(0, 10)
+            interleave(0, 8)
+            quant_k(0, 2)
+            turn_x(0, 2)
+            turn_x(0, 3)
+            interleave(0, 6)
+            quant_x(0, 0)
+            interleave(0, 10)
+            quant_x(0, 1)
+            quant_k(0, 4)
+            quant_x(0, 2)
+            make_beta()
+            quant_x(0, 3)
+            quant_k(0, 8)
+            widen(0, 12)
+            interleave(0, 12)
+            for t in range(PACK):
+                values(0, 0, t)
+            quant_k(0, 10)
+            for t in range(PACK):
+                subtract(0, 0, t)
+                values(0, 1, t)
+            widen(0, 14)
+            interleave(0, 14)
+            quant_k(0, 6)
+            scale_dv(0, 0, 0)
+            scale_dv(0, 0, 1)
+            quant_dv(0, 0, 0)
+            quant_k(0, 12)
+            quant_dv(0, 0, 1)
+            update(0, 0, 0)
+            update(0, 0, 1)
+            for t in range(PACK):
+                subtract(0, 1, t)
+            for t in range(PACK):
+                turn_x(1, t)
+            finish(0, 0, 0)
+            scale_dv(0, 1, 0)
+            quant_k(0, 14)
+            scale_dv(0, 1, 1)
+            quant_dv(0, 1, 0)
+            finish(0, 0, 1)
+            quant_dv(0, 1, 1)
+            update(0, 1, 0)
+            update(0, 1, 1)
+            for t in range(PACK):
+                quant_x(1, t)
+                values(1, 0, t)
+            for h in (0, 2, 4, 6):
+                widen(1, h)
+                interleave(1, h)
+            quant_k(1, 0)
+            for t in range(PACK):
+                subtract(1, 0, t)
+                values(1, 1, t)
+            finish(0, 1, 0)
+            quant_k(1, 2)
+            scale_dv(1, 0, 0)
+            finish(0, 1, 1)
+            scale_dv(1, 0, 1)
+            quant_dv(1, 0, 0)
+            quant_k(1, 4)
+            quant_dv(1, 0, 1)
+            update(1, 0, 0)
+            for h in (8, 10, 12, 14):
+                widen(1, h)
+                interleave(1, h)
+            for t in range(2):
+                subtract(1, 1, t)
+            quant_k(1, 6)
+            update(1, 0, 1)
+            for t in range(2, 4):
+                subtract(1, 1, t)
+            finish(1, 0, 0)
+            quant_k(1, 8)
+            scale_dv(1, 1, 0)
+            finish(1, 0, 1)
+            quant_k(1, 10)
+            quant_dv(1, 1, 0)
+            scale_dv(1, 1, 1)
+            update(1, 1, 0)
+            quant_k(1, 12)
+            quant_dv(1, 1, 1)
+            finish(1, 1, 0)
+            quant_k(1, 14)
+            update(1, 1, 1)
+            finish(1, 1, 1)
+
+        with tc.manual_schedule():
+            body()

@@ -18,10 +18,13 @@ B, N, D, H, DH = 2, 512, 1024, 16, 64
 S = 2 * DH
 P = 128
 PACK = 4
+RUN = 4
 FLOPS = 2 * B * N * D * H * DH + 2 * B * H * N * S * DH
 
-WIDEN_ON_VECTOR = ((0, 0), (0, 2), (0, 8), (0, 10))
-INTERLEAVE_ON_VECTOR = ((0, 0), (0, 2), (0, 8), (0, 10))
+WIDEN_ON_VECTOR = ((0, 0), (0, 2), (0, 6), (0, 8))
+INTERLEAVE_ON_VECTOR = ((0, 2), (0, 8))
+INTERLEAVE_ON_TENSOR = ((1, 0), (1, 2), (1, 4), (1, 6), (1, 8), (1, 10), (1, 14))
+INTERLEAVE_ON_GPSIMD = ()
 
 
 def tile_dpfpattention_pb_w4_kernel(tc, x, wv_words, wv_scales, beta, vo, k_phi_bytes, k_phi_scale, W, out):
@@ -40,10 +43,12 @@ def tile_dpfpattention_pb_w4_kernel(tc, x, wv_words, wv_scales, beta, vo, k_phi_
         nc.gpsimd.memset(wsc[:].rearrange("p g n -> p (g n)").bitcast(I32), 0)
         beta_rows = keep.tile([P, N], BF16, align_bytes=64, name="beta_rows")
         nc.gpsimd.memset(beta_rows[:], 0.0)
+        ident_bf = keep.tile([P, P], BF16, align_bytes=64, name="ident_bf")
+        make_identity(nc, ident_bf[:])
 
         kscale = keep.tile([P, PACK], F32, name="kscale")
         nc.sync.dma_start(out=kscale[:], in_=k_phi_scale.rearrange("a c (p t) f -> p (a c t f)", t=PACK))
-        kb = {}
+        kb, xs, vos, ws = {}, {}, {}, {}
 
         def load_kphi(b, h0, nh):
             kbt = keep.tile([P, nh, PACK * S], U8, align_bytes=64, name=f"kb_{b}_{h0}")
@@ -51,79 +56,93 @@ def tile_dpfpattention_pb_w4_kernel(tc, x, wv_words, wv_scales, beta, vo, k_phi_
             for h in range(nh):
                 kb[b, h0 + h] = kbt[:, h, :]
 
-        xs = {}
-
         def load_x(b, t):
-            xt_ = keep.tile([P, D], BF16, align_bytes=64, name=f"x_{b}_{t}")
-            nc.sync.dma_start(out=xt_[:], in_=x[b].rearrange("(p t) k -> p t k", t=PACK)[:, t, :])
-            xs[b, t] = xt_
-
-        vos = {}
+            xt = keep.tile([P, D], BF16, align_bytes=64, name=f"x_{b}_{t}")
+            nc.sync.dma_start(out=xt[:], in_=x[b].rearrange("(p t) k -> p t k", t=PACK)[:, t, :])
+            xs[b, t] = xt
 
         def load_vo(b, u):
-            v_ = keep.tile([P, 8, PACK, DH], BF16, align_bytes=64, name=f"vo_{b}_{u}")
+            v = keep.tile([P, 8, PACK, DH], BF16, align_bytes=64, name=f"vo_{b}_{u}")
             nc.sync.dma_start(
-                out=v_[:].rearrange("p h t d -> p h (t d)"),
+                out=v[:].rearrange("p h t d -> p h (t d)"),
                 in_=vo[b, 8 * u : 8 * u + 8].rearrange("h (p t) d -> p h (t d)", t=PACK),
             )
-            vos[b, u] = v_
-
-        ws = {}
+            vos[b, u] = v
 
         def load_W(b):
-            w_ = keep.tile([P, H, DH], BF16, align_bytes=64, name=f"W_{b}")
-            nc.sync.dma_start(out=w_[:], in_=W[b].rearrange("h s d -> s h d"))
-            ws[b] = w_
+            w = keep.tile([P, H, DH], BF16, align_bytes=64, name=f"W_{b}")
+            nc.sync.dma_start(out=w[:], in_=W[b].rearrange("h s d -> s h d"))
+            ws[b] = w
 
-        load_kphi(0, 0, 2)
-        load_kphi(0, 4, 2)
-        load_kphi(0, 2, 2)
-        load_kphi(0, 8, 2)
-        for t in range(PACK):
-            load_x(0, t)
-        load_kphi(0, 10, 2)
-        load_kphi(0, 6, 2)
-        for q in range(4):
-            nc.sync.dma_start(
-                out=wsc[32 * q : 32 * q + 4, :, :].bitcast(I32),
-                in_=wv_scales[:, 4 * q : 4 * q + 4, :].rearrange("g q n -> q g n").bitcast(I32),
-            )
-        nc.sync.dma_start(out=beta_rows[0 : B * H, :], in_=beta.rearrange("b h n -> (b h) n"))
         ww = keep.tile([P, 2, 2 * D], U8, align_bytes=64, name="ww")
-        nc.sync.dma_start(out=ww[:], in_=wv_words.rearrange("g p n -> p g n"))
-        load_vo(0, 0)
-        load_kphi(0, 12, 4)
-        load_vo(0, 1)
-        for t in range(PACK):
-            load_x(1, t)
-        load_kphi(1, 0, 8)
+
+        def load_weight():
+            for q in range(4):
+                nc.sync.dma_start(
+                    out=wsc[32 * q : 32 * q + 4, :, :].bitcast(I32),
+                    in_=wv_scales[:, 4 * q : 4 * q + 4, :].rearrange("g q n -> q g n").bitcast(I32),
+                )
+            nc.sync.dma_start(out=beta_rows[0 : B * H, :], in_=beta.rearrange("b h n -> (b h) n"))
+            nc.sync.dma_start(out=ww[:], in_=wv_words.rearrange("g p n -> p g n"))
+
+        load_kphi(0,4,2)
+        load_kphi(0,8,2)
+        load_kphi(0,2,2)
+        load_x(0,0)
+        load_x(0,3)
+        load_kphi(0,6,2)
+        load_x(0,1)
+        load_x(0,2)
+        load_kphi(0,0,2)
+        load_weight()
+        load_vo(0,0)
+        load_kphi(0,10,2)
+        load_vo(0,1)
+        load_kphi(1,0,4)
         load_W(0)
-        load_vo(1, 0)
-        load_kphi(1, 8, 8)
-        load_vo(1, 1)
+        load_kphi(0,12,4)
+        load_x(1,0)
+        load_x(1,1)
+        load_x(1,3)
+        load_x(1,2)
+        load_vo(1,0)
+        load_kphi(1,4,4)
+        load_kphi(1,8,8)
+        load_vo(1,1)
         load_W(1)
 
-        beta_t = keep.tile([P, B * H, PACK], BF16, align_bytes=64, name="beta_t")
+        beta_t = keep.tile([P, B * H, PACK, RUN], BF16, align_bytes=64, name="beta_t")
 
-        def make_beta():
-            bt = psum.tile([P, 2, P], F32, name="xt", bufs=2)
+        betas = []
+
+        def turn_beta():
+            bt = psum.tile([P, 2, P], F32, name="turn", bufs=3)
             words = beta_rows[:].bitcast(F32)
             for u in range(2):
                 nc.tensor.transpose(bt[:, u, :], words[:, u : 2 * P : 2], ident[:])
-            nc.vector.tensor_copy(
-                out=beta_t[:].rearrange("p r t -> p (r t)").bitcast(F32).rearrange("p (r u) -> p r u", u=2),
-                in_=bt[:, :, 0 : B * H].rearrange("p u r -> p r u"),
-            )
+            betas.append(bt)
 
-        xg, xc = {}, {}
+        def copy_beta():
+            for u in range(2):
+                pair = betas[0][:, u, 0 : B * H].bitcast(BF16).rearrange("p (r e) -> p r e", e=2)
+                nc.scalar.copy(
+                    out=beta_t[:, :, 2 * u : 2 * u + 2, :],
+                    in_=pair.unsqueeze(3).to_broadcast([P, B * H, 2, RUN]),
+                )
+
+        xp, xg, xc = {}, {}, {}
 
         def turn_x(b, t):
-            ps = psum.tile([P, 2, 2, P], F32, name="xt", bufs=2)
+            ps = psum.tile([P, 2, 2, P], F32, name="turn", bufs=3)
             words = xs[b, t][:].bitcast(F32)
             for g in range(2):
                 for u in range(2):
                     nc.tensor.transpose(ps[:, g, u, :], words[:, 256 * g + u : 256 * (g + 1) : 2], ident[:])
-            gt = work.tile([P, 2 * P * PACK], BF16, align_bytes=64, name="xg", bufs=4)
+            xp[b, t] = ps
+
+        def copy_x(b, t):
+            ps = xp[b, t]
+            gt = work.tile([P, 2 * P * PACK], BF16, align_bytes=64, name="xg", bufs=8)
             nc.scalar.copy(
                 out=gt[:].bitcast(F32).rearrange("p (g r u) -> p g r u", g=2, u=2),
                 in_=ps[:].rearrange("p g u r -> p g r u"),
@@ -143,7 +162,7 @@ def tile_dpfpattention_pb_w4_kernel(tc, x, wv_words, wv_scales, beta, vo, k_phi_
         planes, inter, kc = {}, {}, {}
 
         def widen(b, h):
-            pl = work.tile([P, 2, PACK, S], BF16, align_bytes=64, name="planes", bufs=6)
+            pl = work.tile([P, 2, PACK, S], BF16, align_bytes=64, name="planes", bufs=16)
             for i in range(2):
                 for t in range(PACK):
                     src = kb[b, h + i][:, S * t : S * (t + 1)].bitcast(FP8)
@@ -153,10 +172,37 @@ def tile_dpfpattention_pb_w4_kernel(tc, x, wv_words, wv_scales, beta, vo, k_phi_
                         nc.scalar.activation(out=pl[:, i, t, :], in_=src, func=ACT.Copy, scale=kscale[:, t : t + 1])
             planes[b, h] = pl
 
+        ips = {}
+
+        def interleave_tensor(b, h):
+            pl = planes[b, h]
+            ps = psum.tile([P, 2, S * PACK], BF16, name="turn", bufs=3)
+            for i in range(2):
+                nc.tensor.matmul(
+                    ps[:, i, :], lhsT=ident_bf[:], rhs=pl[:, i, :, :].rearrange("p t s -> p s t"), start=True, stop=True
+                )
+            ips[b, h] = ps
+
         def interleave(b, h):
-            it = work.tile([P, 2, S, PACK], BF16, align_bytes=64, name="inter", bufs=6)
-            copy = nc.vector.tensor_copy if (b, h) in INTERLEAVE_ON_VECTOR else nc.scalar.copy
-            copy(out=it[:], in_=planes[b, h][:].rearrange("p h t s -> p h s t"))
+            pl = planes[b, h]
+            if (b, h) in INTERLEAVE_ON_GPSIMD:
+                it = work.tile([P, 2, S, PACK], BF16, align_bytes=64, name="inter", bufs=16)
+                for i in range(2):
+                    nc.gpsimd.tensor_scalar(
+                        out=it[:, i, :, :], in0=pl[:, i, :, :].rearrange("p t s -> p s t"), scalar1=1.0, scalar2=0.0, op0=ALU.mult, op1=ALU.add
+                    )
+                inter[b, h] = it
+                return
+            it = work.tile([P, 2, S, PACK], BF16, align_bytes=64, name="inter", bufs=16)
+            if (b, h) in INTERLEAVE_ON_TENSOR:
+                nc.scalar.copy(out=it[:].rearrange("p h s t -> p h (s t)"), in_=ips[b, h][:])
+            else:
+                copy = nc.vector.tensor_copy if (b, h) in INTERLEAVE_ON_VECTOR else nc.scalar.copy
+                for i in range(2):
+                    copy(
+                        out=it[:, i, :, :].rearrange("p (c i) t -> p c t i", i=RUN),
+                        in_=pl[:, i, :, :].rearrange("p t (c i) -> p c t i", i=RUN),
+                    )
             inter[b, h] = it
 
         def quant_k(b, h):
@@ -173,7 +219,7 @@ def tile_dpfpattention_pb_w4_kernel(tc, x, wv_words, wv_scales, beta, vo, k_phi_
         vps, t1s, dvg, dvc = {}, {}, {}, {}
 
         def values(b, u, t):
-            ps = psum.tile([P, 512], F32, name="v", bufs=4)
+            ps = psum.tile([P, 512], F32, name="v", bufs=3)
             codes, scales = xc[b, t]
             for g in range(2):
                 nc.tensor.matmul_mx(
@@ -188,166 +234,204 @@ def tile_dpfpattention_pb_w4_kernel(tc, x, wv_words, wv_scales, beta, vo, k_phi_
             vps[b, u, t] = ps
 
         def subtract(b, u, t):
-            if t == 0:
-                t1 = work.tile([P, PACK, 8, DH], F32, align_bytes=64, name="t1", bufs=2)
+            if (b, u) not in t1s:
+                t1 = work.tile([P, 8, DH // RUN, PACK, RUN], F32, align_bytes=64, name="t1", bufs=3)
                 t1s[b, u] = t1
             nc.vector.tensor_tensor(
-                out=t1s[b, u][:, t, :, :],
-                in0=vps[b, u, t][:].rearrange("p (h d) -> p h d", d=DH),
-                in1=vos[b, u][:, :, t, :],
+                out=t1s[b, u][:, :, :, t, :],
+                in0=vps[b, u, t][:].rearrange("p (h c i) -> p h c i", h=8, i=RUN),
+                in1=vos[b, u][:, :, t, :].rearrange("p h (c i) -> p h c i", i=RUN),
                 op=ALU.subtract,
             )
 
-        def scale_dv(b, u, i):
+        def scale_dv(b, u, j):
             dg = work.tile([P, 4, DH, PACK], BF16, align_bytes=64, name="dvg", bufs=3)
-            r0 = 16 * b + 8 * u + 4 * i
+            r0 = 16 * b + 8 * u + 4 * j
             nc.vector.tensor_tensor(
-                out=dg[:],
-                in0=t1s[b, u][:, :, 4 * i : 4 * i + 4, :].rearrange("p t h d -> p h d t"),
-                in1=beta_t[:, r0 : r0 + 4, :].unsqueeze(2).to_broadcast([P, 4, DH, PACK]),
+                out=dg[:].rearrange("p h (c i) t -> p h c t i", i=RUN),
+                in0=t1s[b, u][:, 4 * j : 4 * j + 4, :, :, :],
+                in1=beta_t[:, r0 : r0 + 4, :, :].unsqueeze(2).to_broadcast([P, 4, DH // RUN, PACK, RUN]),
                 op=ALU.mult,
             )
-            dvg[b, u, i] = dg
+            dvg[b, u, j] = dg
 
-        def quant_dv(b, u, i):
+        def quant_dv(b, u, j):
             codes = work.tile([P, 4, DH], U32, align_bytes=64, name="dvc", bufs=4)
             scales = work.tile([P, 4, DH], U8, align_bytes=64, name="dvsc", bufs=4)
             nc.vector.quantize_mx(
                 out=codes[:].rearrange("p h d -> p (h d)").bitcast(E4M3X4),
                 scales=scales[:].rearrange("p h d -> p (h d)"),
-                in_=dvg[b, u, i][:].rearrange("p h d t -> p (h d t)"),
+                in_=dvg[b, u, j][:].rearrange("p h d t -> p (h d t)"),
             )
-            dvc[b, u, i] = (codes, scales)
+            dvc[b, u, j] = (codes, scales)
 
         ops = {}
 
-        def update(b, u, i):
+        def update(b, u, j):
             ps = psum.tile([P, 4, DH], F32, name="o", bufs=2)
-            dcodes, dscales = dvc[b, u, i]
-            for j in range(4):
-                kcodes, kscales = kc[b, 8 * u + 4 * i + j]
+            dcodes, dscales = dvc[b, u, j]
+            for i in range(4):
+                kcodes, kscales = kc[b, 8 * u + 4 * j + i // 2 * 2 + i % 2]
                 nc.tensor.matmul_mx(
-                    out=ps[:, j, :],
+                    out=ps[:, i, :],
                     lhsT=kcodes.bitcast(E4M3X4),
                     lhsT_scale=kscales,
-                    rhs=dcodes[:, j, :].bitcast(E4M3X4),
-                    rhs_scale=dscales[:, j, :],
+                    rhs=dcodes[:, i, :].bitcast(E4M3X4),
+                    rhs_scale=dscales[:, i, :],
                     start=True,
                     stop=True,
                 )
-            ops[b, u, i] = ps
+            ops[b, u, j] = ps
 
-        def finish(b, u, i):
-            h0 = 8 * u + 4 * i
+        def finish(b, u, j):
+            h0 = 8 * u + 4 * j
             ot = work.tile([P, 4, DH], F32, align_bytes=64, name="ot", bufs=4)
-            nc.vector.tensor_tensor(out=ot[:], in0=ops[b, u, i][:], in1=ws[b][:, h0 : h0 + 4, :], op=ALU.add)
+            nc.vector.tensor_tensor(out=ot[:], in0=ops[b, u, j][:], in1=ws[b][:, h0 : h0 + 4, :], op=ALU.add)
             nc.sync.dma_start(out=out[b, h0 : h0 + 4].rearrange("h s d -> s h d"), in_=ot[:])
 
-        def kphi(b, h):
-            widen(b, h)
-            interleave(b, h)
-            quant_k(b, h)
-
-
-        def body():
-            widen(0, 0)
+        with tc.manual_schedule():
             widen(0, 4)
+            widen(0, 8)
             widen(0, 2)
             interleave(0, 4)
-            interleave(0, 0)
-            widen(0, 8)
-            interleave(0, 2)
-            quant_k(0, 0)
             turn_x(0, 0)
+            interleave(0, 8)
+            turn_x(0, 3)
+            interleave(0, 2)
+            copy_x(0, 0)
+            quant_k(0, 8)
+            copy_x(0, 3)
             turn_x(0, 1)
             widen(0, 6)
-            widen(0, 10)
-            interleave(0, 8)
-            quant_k(0, 2)
             turn_x(0, 2)
-            turn_x(0, 3)
-            interleave(0, 6)
+            copy_x(0, 1)
             quant_x(0, 0)
-            interleave(0, 10)
+            quant_x(0, 3)
+            interleave(0, 6)
             quant_x(0, 1)
             quant_k(0, 4)
-            quant_x(0, 2)
-            make_beta()
-            quant_x(0, 3)
-            quant_k(0, 8)
-            widen(0, 12)
-            interleave(0, 12)
-            for t in range(PACK):
-                values(0, 0, t)
-            quant_k(0, 10)
-            for t in range(PACK):
-                subtract(0, 0, t)
-                values(0, 1, t)
-            widen(0, 14)
-            interleave(0, 14)
+            widen(0, 0)
+            turn_beta()
+            copy_x(0, 2)
+            quant_k(0, 2)
             quant_k(0, 6)
-            scale_dv(0, 0, 0)
+            copy_beta()
+            quant_x(0, 2)
+            interleave(0, 0)
+            values(0, 0, 0)
+            values(0, 0, 2)
+            values(0, 0, 3)
+            quant_k(0, 0)
+            subtract(0, 0, 2)
+            widen(0, 10)
+            subtract(0, 0, 3)
+            values(0, 0, 1)
+            subtract(0, 0, 0)
+            values(0, 1, 2)
+            subtract(0, 0, 1)
+            values(0, 1, 1)
+            interleave(0, 10)
+            subtract(0, 1, 2)
+            values(0, 1, 3)
             scale_dv(0, 0, 1)
+            values(0, 1, 0)
+            widen(1, 0)
+            subtract(0, 1, 3)
+            widen(1, 2)
+            scale_dv(0, 0, 0)
+            interleave_tensor(1, 0)
+            quant_k(0, 10)
+            interleave(1, 0)
+            interleave_tensor(1, 2)
             quant_dv(0, 0, 0)
-            quant_k(0, 12)
-            quant_dv(0, 0, 1)
+            subtract(0, 1, 1)
+            widen(0, 14)
             update(0, 0, 0)
-            update(0, 0, 1)
-            for t in range(PACK):
-                subtract(0, 1, t)
-            for t in range(PACK):
-                turn_x(1, t)
+            turn_x(1, 0)
+            subtract(0, 1, 0)
             finish(0, 0, 0)
-            scale_dv(0, 1, 0)
-            quant_k(0, 14)
+            turn_x(1, 1)
+            interleave(1, 2)
             scale_dv(0, 1, 1)
-            quant_dv(0, 1, 0)
-            finish(0, 0, 1)
+            copy_x(1, 0)
+            turn_x(1, 3)
+            copy_x(1, 1)
+            quant_dv(0, 0, 1)
+            turn_x(1, 2)
             quant_dv(0, 1, 1)
-            update(0, 1, 0)
-            update(0, 1, 1)
-            for t in range(PACK):
-                quant_x(1, t)
-                values(1, 0, t)
-            for h in (0, 2, 4, 6):
-                widen(1, h)
-                interleave(1, h)
+            copy_x(1, 3)
+            quant_x(1, 1)
+            update(0, 0, 1)
             quant_k(1, 0)
-            for t in range(PACK):
-                subtract(1, 0, t)
-                values(1, 1, t)
-            finish(0, 1, 0)
+            copy_x(1, 2)
+            values(1, 0, 1)
+            quant_x(1, 3)
+            finish(0, 0, 1)
+            widen(0, 12)
+            values(1, 0, 3)
+            quant_x(1, 2)
+            subtract(1, 0, 1)
+            values(1, 1, 3)
+            subtract(1, 0, 3)
+            values(1, 0, 2)
+            widen(1, 4)
+            quant_x(1, 0)
+            values(1, 1, 1)
+            subtract(1, 0, 2)
+            scale_dv(0, 1, 0)
+            interleave(0, 12)
+            values(1, 0, 0)
+            interleave_tensor(1, 4)
             quant_k(1, 2)
-            scale_dv(1, 0, 0)
-            finish(0, 1, 1)
+            widen(1, 10)
+            quant_dv(0, 1, 0)
+            quant_k(0, 12)
+            update(0, 1, 0)
+            subtract(1, 1, 3)
+            widen(1, 14)
+            finish(0, 1, 0)
+            values(1, 1, 0)
+            subtract(1, 1, 1)
+            interleave_tensor(1, 10)
+            subtract(1, 1, 0)
+            values(1, 1, 2)
+            interleave(0, 14)
+            subtract(1, 0, 0)
+            interleave_tensor(1, 14)
+            subtract(1, 1, 2)
             scale_dv(1, 0, 1)
+            interleave(1, 14)
+            widen(1, 6)
+            quant_k(0, 14)
+            scale_dv(1, 0, 0)
+            update(0, 1, 1)
+            widen(1, 12)
+            interleave_tensor(1, 6)
+            finish(0, 1, 1)
             quant_dv(1, 0, 0)
-            quant_k(1, 4)
+            interleave(1, 6)
             quant_dv(1, 0, 1)
             update(1, 0, 0)
-            for h in (8, 10, 12, 14):
-                widen(1, h)
-                interleave(1, h)
-            for t in range(2):
-                subtract(1, 1, t)
-            quant_k(1, 6)
-            update(1, 0, 1)
-            for t in range(2, 4):
-                subtract(1, 1, t)
-            finish(1, 0, 0)
-            quant_k(1, 8)
-            scale_dv(1, 1, 0)
-            finish(1, 0, 1)
-            quant_k(1, 10)
-            quant_dv(1, 1, 0)
-            scale_dv(1, 1, 1)
-            update(1, 1, 0)
-            quant_k(1, 12)
-            quant_dv(1, 1, 1)
-            finish(1, 1, 0)
             quant_k(1, 14)
+            interleave(1, 4)
+            finish(1, 0, 0)
+            quant_k(1, 6)
+            interleave(1, 10)
+            quant_k(1, 4)
+            scale_dv(1, 1, 1)
+            update(1, 0, 1)
+            widen(1, 8)
+            quant_k(1, 10)
+            interleave(1, 12)
+            quant_dv(1, 1, 1)
+            interleave_tensor(1, 8)
+            finish(1, 0, 1)
+            scale_dv(1, 1, 0)
+            interleave(1, 8)
+            quant_k(1, 12)
+            quant_dv(1, 1, 0)
             update(1, 1, 1)
+            quant_k(1, 8)
             finish(1, 1, 1)
-
-        with tc.manual_schedule():
-            body()
+            update(1, 1, 0)
+            finish(1, 1, 0)

@@ -21,10 +21,8 @@ PACK = 4
 RUN = 4
 FLOPS = 2 * B * N * D * H * DH + 2 * B * H * N * S * DH
 
-WIDEN_ON_VECTOR = ((0, 0), (0, 2), (0, 6), (0, 8))
-INTERLEAVE_ON_VECTOR = ((0, 2), (0, 8))
-INTERLEAVE_ON_TENSOR = ((1, 0), (1, 2), (1, 4), (1, 6), (1, 8), (1, 10), (1, 14))
-INTERLEAVE_ON_GPSIMD = ()
+WIDEN_ON_VECTOR = ((0, 0), (0, 4), (0, 6), (0, 10))
+INTERLEAVE_ON_VECTOR = ((0, 0), (0, 4), (0, 6), (1, 0))
 
 
 def tile_dpfpattention_pb_w4_kernel(tc, x, wv_words, wv_scales, beta, vo, k_phi_bytes, k_phi_scale, W, out):
@@ -35,17 +33,15 @@ def tile_dpfpattention_pb_w4_kernel(tc, x, wv_words, wv_scales, beta, vo, k_phi_
         psum = ctx.enter_context(tc.psum_pool(name="psum", bufs=2))
 
         warm = keep.tile([P, 1], F32, name="warm")
-        nc.gpsimd.memset(warm[:], 0.0)
+        nc.vector.memset(warm[:], 0.0)
         nc.scalar.activation(out=warm[:], in_=warm[:], func=ACT.Copy)
+        wsc = keep.tile([P, 2, D], U8, align_bytes=64, name="wsc")
+        nc.vector.memset(wsc[:].rearrange("p g n -> p (g n)").bitcast(I32), 0)
         ident = keep.tile([P, P], F32, name="ident")
         make_identity(nc, ident[:])
-        wsc = keep.tile([P, 2, D], U8, align_bytes=64, name="wsc")
-        nc.gpsimd.memset(wsc[:].rearrange("p g n -> p (g n)").bitcast(I32), 0)
         beta_rows = keep.tile([P, N], BF16, align_bytes=64, name="beta_rows")
         nc.gpsimd.memset(beta_rows[:], 0.0)
-        ident_bf = keep.tile([P, P], BF16, align_bytes=64, name="ident_bf")
-        make_identity(nc, ident_bf[:])
-
+        nc.gpsimd.dma_start(out=beta_rows[0 : B * H, :], in_=beta.rearrange("b h n -> (b h) n"))
         kscale = keep.tile([P, PACK], F32, name="kscale")
         nc.sync.dma_start(out=kscale[:], in_=k_phi_scale.rearrange("a c (p t) f -> p (a c t f)", t=PACK))
         kb, xs, vos, ws = {}, {}, {}, {}
@@ -56,10 +52,11 @@ def tile_dpfpattention_pb_w4_kernel(tc, x, wv_words, wv_scales, beta, vo, k_phi_
             for h in range(nh):
                 kb[b, h0 + h] = kbt[:, h, :]
 
-        def load_x(b, t):
-            xt = keep.tile([P, D], BF16, align_bytes=64, name=f"x_{b}_{t}")
-            nc.sync.dma_start(out=xt[:], in_=x[b].rearrange("(p t) k -> p t k", t=PACK)[:, t, :])
-            xs[b, t] = xt
+        def load_x(b, t0, nt):
+            xt = keep.tile([P, nt, D], BF16, align_bytes=64, name=f"x_{b}_{t0}")
+            nc.sync.dma_start(out=xt[:], in_=x[b].rearrange("(p t) k -> p t k", t=PACK)[:, t0 : t0 + nt, :])
+            for t in range(nt):
+                xs[b, t0 + t] = xt[:, t, :]
 
         def load_vo(b, u):
             v = keep.tile([P, 8, PACK, DH], BF16, align_bytes=64, name=f"vo_{b}_{u}")
@@ -76,40 +73,38 @@ def tile_dpfpattention_pb_w4_kernel(tc, x, wv_words, wv_scales, beta, vo, k_phi_
 
         ww = keep.tile([P, 2, 2 * D], U8, align_bytes=64, name="ww")
 
-        def load_weight():
+        def load_weight_scales():
             for q in range(4):
                 nc.sync.dma_start(
                     out=wsc[32 * q : 32 * q + 4, :, :].bitcast(I32),
                     in_=wv_scales[:, 4 * q : 4 * q + 4, :].rearrange("g q n -> q g n").bitcast(I32),
                 )
-            nc.sync.dma_start(out=beta_rows[0 : B * H, :], in_=beta.rearrange("b h n -> (b h) n"))
+
+        def load_weight():
             nc.sync.dma_start(out=ww[:], in_=wv_words.rearrange("g p n -> p g n"))
 
-        load_kphi(0,4,2)
-        load_kphi(0,8,2)
         load_kphi(0,2,2)
-        load_x(0,0)
-        load_x(0,3)
         load_kphi(0,6,2)
-        load_x(0,1)
-        load_x(0,2)
+        load_kphi(0,8,2)
         load_kphi(0,0,2)
+        load_kphi(0,4,2)
+        load_x(0,2,2)
+        load_x(0,0,2)
         load_weight()
-        load_vo(0,0)
+        load_weight_scales()
         load_kphi(0,10,2)
-        load_vo(0,1)
-        load_kphi(1,0,4)
-        load_W(0)
-        load_kphi(0,12,4)
-        load_x(1,0)
-        load_x(1,1)
-        load_x(1,3)
-        load_x(1,2)
-        load_vo(1,0)
+        load_vo(0,0)
         load_kphi(1,4,4)
-        load_kphi(1,8,8)
+        load_vo(0,1)
+        load_kphi(0,12,4)
+        load_x(1,0,4)
+        load_kphi(1,0,4)
+        load_vo(1,0)
         load_vo(1,1)
+        load_kphi(1,8,4)
         load_W(1)
+        load_W(0)
+        load_kphi(1,12,4)
 
         beta_t = keep.tile([P, B * H, PACK, RUN], BF16, align_bytes=64, name="beta_t")
 
@@ -134,7 +129,7 @@ def tile_dpfpattention_pb_w4_kernel(tc, x, wv_words, wv_scales, beta, vo, k_phi_
 
         def turn_x(b, t):
             ps = psum.tile([P, 2, 2, P], F32, name="turn", bufs=3)
-            words = xs[b, t][:].bitcast(F32)
+            words = xs[b, t].bitcast(F32)
             for g in range(2):
                 for u in range(2):
                     nc.tensor.transpose(ps[:, g, u, :], words[:, 256 * g + u : 256 * (g + 1) : 2], ident[:])
@@ -172,37 +167,15 @@ def tile_dpfpattention_pb_w4_kernel(tc, x, wv_words, wv_scales, beta, vo, k_phi_
                         nc.scalar.activation(out=pl[:, i, t, :], in_=src, func=ACT.Copy, scale=kscale[:, t : t + 1])
             planes[b, h] = pl
 
-        ips = {}
-
-        def interleave_tensor(b, h):
-            pl = planes[b, h]
-            ps = psum.tile([P, 2, S * PACK], BF16, name="turn", bufs=3)
-            for i in range(2):
-                nc.tensor.matmul(
-                    ps[:, i, :], lhsT=ident_bf[:], rhs=pl[:, i, :, :].rearrange("p t s -> p s t"), start=True, stop=True
-                )
-            ips[b, h] = ps
-
         def interleave(b, h):
             pl = planes[b, h]
-            if (b, h) in INTERLEAVE_ON_GPSIMD:
-                it = work.tile([P, 2, S, PACK], BF16, align_bytes=64, name="inter", bufs=16)
-                for i in range(2):
-                    nc.gpsimd.tensor_scalar(
-                        out=it[:, i, :, :], in0=pl[:, i, :, :].rearrange("p t s -> p s t"), scalar1=1.0, scalar2=0.0, op0=ALU.mult, op1=ALU.add
-                    )
-                inter[b, h] = it
-                return
             it = work.tile([P, 2, S, PACK], BF16, align_bytes=64, name="inter", bufs=16)
-            if (b, h) in INTERLEAVE_ON_TENSOR:
-                nc.scalar.copy(out=it[:].rearrange("p h s t -> p h (s t)"), in_=ips[b, h][:])
-            else:
-                copy = nc.vector.tensor_copy if (b, h) in INTERLEAVE_ON_VECTOR else nc.scalar.copy
-                for i in range(2):
-                    copy(
-                        out=it[:, i, :, :].rearrange("p (c i) t -> p c t i", i=RUN),
-                        in_=pl[:, i, :, :].rearrange("p t (c i) -> p c t i", i=RUN),
-                    )
+            copy = nc.vector.tensor_copy if (b, h) in INTERLEAVE_ON_VECTOR else nc.scalar.copy
+            for i in range(2):
+                copy(
+                    out=it[:, i, :, :].rearrange("p (c i) t -> p c t i", i=RUN),
+                    in_=pl[:, i, :, :].rearrange("p t (c i) -> p c t i", i=RUN),
+                )
             inter[b, h] = it
 
         def quant_k(b, h):
@@ -290,148 +263,141 @@ def tile_dpfpattention_pb_w4_kernel(tc, x, wv_words, wv_scales, beta, vo, k_phi_
             nc.sync.dma_start(out=out[b, h0 : h0 + 4].rearrange("h s d -> s h d"), in_=ot[:])
 
         with tc.manual_schedule():
-            widen(0, 4)
-            widen(0, 8)
             widen(0, 2)
-            interleave(0, 4)
-            turn_x(0, 0)
-            interleave(0, 8)
-            turn_x(0, 3)
-            interleave(0, 2)
-            copy_x(0, 0)
-            quant_k(0, 8)
-            copy_x(0, 3)
-            turn_x(0, 1)
             widen(0, 6)
-            turn_x(0, 2)
-            copy_x(0, 1)
-            quant_x(0, 0)
-            quant_x(0, 3)
+            widen(0, 8)
             interleave(0, 6)
-            quant_x(0, 1)
-            quant_k(0, 4)
             widen(0, 0)
+            interleave(0, 2)
             turn_beta()
-            copy_x(0, 2)
-            quant_k(0, 2)
+            widen(0, 4)
+            turn_x(0, 3)
             quant_k(0, 6)
-            copy_beta()
-            quant_x(0, 2)
+            interleave(0, 4)
+            interleave(0, 8)
+            turn_x(0, 2)
+            quant_k(0, 2)
+            quant_k(0, 4)
+            copy_x(0, 3)
             interleave(0, 0)
-            values(0, 0, 0)
-            values(0, 0, 2)
-            values(0, 0, 3)
+            copy_x(0, 2)
+            turn_x(0, 1)
+            quant_k(0, 8)
             quant_k(0, 0)
-            subtract(0, 0, 2)
+            copy_beta()
+            turn_x(0, 0)
+            quant_x(0, 2)
+            copy_x(0, 1)
+            quant_x(0, 3)
+            quant_x(0, 1)
+            copy_x(0, 0)
+            values(0, 0, 2)
             widen(0, 10)
-            subtract(0, 0, 3)
+            values(0, 0, 3)
+            quant_x(0, 0)
+            interleave(0, 10)
             values(0, 0, 1)
+            subtract(0, 0, 1)
+            subtract(0, 0, 3)
+            values(0, 0, 0)
+            widen(1, 4)
+            subtract(0, 0, 2)
+            values(0, 1, 3)
             subtract(0, 0, 0)
             values(0, 1, 2)
-            subtract(0, 0, 1)
-            values(0, 1, 1)
-            interleave(0, 10)
-            subtract(0, 1, 2)
-            values(0, 1, 3)
+            quant_k(0, 10)
+            widen(1, 6)
             scale_dv(0, 0, 1)
             values(0, 1, 0)
-            widen(1, 0)
-            subtract(0, 1, 3)
-            widen(1, 2)
+            interleave(1, 4)
             scale_dv(0, 0, 0)
-            interleave_tensor(1, 0)
-            quant_k(0, 10)
-            interleave(1, 0)
-            interleave_tensor(1, 2)
+            subtract(0, 1, 2)
+            interleave(1, 6)
             quant_dv(0, 0, 0)
-            subtract(0, 1, 1)
+            values(0, 1, 1)
+            subtract(0, 1, 3)
             widen(0, 14)
             update(0, 0, 0)
+            quant_k(1, 6)
+            subtract(0, 1, 1)
             turn_x(1, 0)
+            quant_dv(0, 0, 1)
+            widen(0, 12)
             subtract(0, 1, 0)
-            finish(0, 0, 0)
             turn_x(1, 1)
-            interleave(1, 2)
+            quant_k(1, 4)
+            turn_x(1, 2)
             scale_dv(0, 1, 1)
             copy_x(1, 0)
-            turn_x(1, 3)
-            copy_x(1, 1)
-            quant_dv(0, 0, 1)
-            turn_x(1, 2)
-            quant_dv(0, 1, 1)
-            copy_x(1, 3)
-            quant_x(1, 1)
             update(0, 0, 1)
-            quant_k(1, 0)
-            copy_x(1, 2)
-            values(1, 0, 1)
-            quant_x(1, 3)
-            finish(0, 0, 1)
-            widen(0, 12)
-            values(1, 0, 3)
-            quant_x(1, 2)
-            subtract(1, 0, 1)
-            values(1, 1, 3)
-            subtract(1, 0, 3)
-            values(1, 0, 2)
-            widen(1, 4)
+            copy_x(1, 1)
+            turn_x(1, 3)
             quant_x(1, 0)
-            values(1, 1, 1)
-            subtract(1, 0, 2)
-            scale_dv(0, 1, 0)
-            interleave(0, 12)
-            values(1, 0, 0)
-            interleave_tensor(1, 4)
-            quant_k(1, 2)
-            widen(1, 10)
-            quant_dv(0, 1, 0)
-            quant_k(0, 12)
-            update(0, 1, 0)
-            subtract(1, 1, 3)
-            widen(1, 14)
-            finish(0, 1, 0)
+            quant_dv(0, 1, 1)
+            copy_x(1, 2)
             values(1, 1, 0)
-            subtract(1, 1, 1)
-            interleave_tensor(1, 10)
+            quant_x(1, 1)
+            copy_x(1, 3)
+            scale_dv(0, 1, 0)
+            values(1, 1, 1)
+            widen(1, 0)
+            values(1, 0, 1)
+            quant_x(1, 2)
+            quant_dv(0, 1, 0)
             subtract(1, 1, 0)
-            values(1, 1, 2)
-            interleave(0, 14)
-            subtract(1, 0, 0)
-            interleave_tensor(1, 14)
-            subtract(1, 1, 2)
-            scale_dv(1, 0, 1)
-            interleave(1, 14)
-            widen(1, 6)
-            quant_k(0, 14)
-            scale_dv(1, 0, 0)
-            update(0, 1, 1)
-            widen(1, 12)
-            interleave_tensor(1, 6)
-            finish(0, 1, 1)
-            quant_dv(1, 0, 0)
-            interleave(1, 6)
-            quant_dv(1, 0, 1)
-            update(1, 0, 0)
-            quant_k(1, 14)
-            interleave(1, 4)
-            finish(1, 0, 0)
-            quant_k(1, 6)
-            interleave(1, 10)
-            quant_k(1, 4)
-            scale_dv(1, 1, 1)
-            update(1, 0, 1)
+            interleave(0, 12)
+            interleave(1, 0)
+            values(1, 0, 2)
+            quant_x(1, 3)
+            widen(1, 10)
+            subtract(1, 0, 1)
+            quant_k(0, 12)
+            values(1, 1, 3)
+            subtract(1, 1, 1)
             widen(1, 8)
-            quant_k(1, 10)
-            interleave(1, 12)
-            quant_dv(1, 1, 1)
-            interleave_tensor(1, 8)
-            finish(1, 0, 1)
-            scale_dv(1, 1, 0)
+            subtract(1, 0, 2)
+            values(1, 0, 3)
+            subtract(1, 1, 3)
+            values(1, 1, 2)
+            interleave(1, 10)
+            subtract(1, 0, 3)
+            values(1, 0, 0)
+            quant_k(1, 0)
+            subtract(1, 1, 2)
             interleave(1, 8)
-            quant_k(1, 12)
-            quant_dv(1, 1, 0)
-            update(1, 1, 1)
+            quant_k(1, 10)
+            finish(0, 0, 1)
+            finish(0, 0, 0)
+            update(0, 1, 0)
+            subtract(1, 0, 0)
+            widen(1, 2)
+            finish(0, 1, 0)
             quant_k(1, 8)
-            finish(1, 1, 1)
+            scale_dv(1, 0, 0)
+            widen(1, 14)
+            scale_dv(1, 0, 1)
+            interleave(1, 2)
+            quant_dv(1, 0, 0)
+            scale_dv(1, 1, 1)
+            interleave(1, 14)
+            quant_k(1, 2)
+            quant_dv(1, 1, 1)
+            widen(1, 12)
+            update(1, 0, 0)
+            quant_dv(1, 0, 1)
+            scale_dv(1, 1, 0)
+            update(1, 0, 1)
+            interleave(0, 14)
+            finish(1, 0, 0)
+            quant_dv(1, 1, 0)
+            finish(1, 0, 1)
             update(1, 1, 0)
+            interleave(1, 12)
+            quant_k(0, 14)
+            quant_k(1, 14)
+            update(0, 1, 1)
             finish(1, 1, 0)
+            finish(0, 1, 1)
+            quant_k(1, 12)
+            update(1, 1, 1)
+            finish(1, 1, 1)

@@ -21,8 +21,8 @@ PACK = 4
 RUN = 4
 FLOPS = 2 * B * N * D * H * DH + 2 * B * H * N * S * DH
 
-WIDEN_ON_VECTOR = ((0, 0), (0, 4), (0, 6), (0, 10))
-INTERLEAVE_ON_VECTOR = ((0, 0), (0, 4), (0, 6), (1, 0))
+WIDEN_ON_VECTOR = ((0, 0), (0, 2), (0, 4), (0, 8), (0, 10))
+INTERLEAVE_ON_VECTOR = ((0, 0), (0, 2), (0, 4), (0, 8), (0, 10))
 
 
 def tile_dpfpattention_pb_w4_kernel(tc, x, wv_words, wv_scales, beta, vo, k_phi_bytes, k_phi_scale, W, out):
@@ -32,15 +32,15 @@ def tile_dpfpattention_pb_w4_kernel(tc, x, wv_words, wv_scales, beta, vo, k_phi_
         work = ctx.enter_context(tc.tile_pool(name="work", bufs=4))
         psum = ctx.enter_context(tc.psum_pool(name="psum", bufs=2))
 
+        ident = keep.tile([P, P], F32, name="ident")
+        make_identity(nc, ident[:])
         warm = keep.tile([P, 1], F32, name="warm")
         nc.vector.memset(warm[:], 0.0)
         nc.scalar.activation(out=warm[:], in_=warm[:], func=ACT.Copy)
         wsc = keep.tile([P, 2, D], U8, align_bytes=64, name="wsc")
         nc.vector.memset(wsc[:].rearrange("p g n -> p (g n)").bitcast(I32), 0)
-        ident = keep.tile([P, P], F32, name="ident")
-        make_identity(nc, ident[:])
         beta_rows = keep.tile([P, N], BF16, align_bytes=64, name="beta_rows")
-        nc.gpsimd.memset(beta_rows[:], 0.0)
+        nc.vector.memset(beta_rows[:], 0.0)
         nc.gpsimd.dma_start(out=beta_rows[0 : B * H, :], in_=beta.rearrange("b h n -> (b h) n"))
         kscale = keep.tile([P, PACK], F32, name="kscale")
         nc.sync.dma_start(out=kscale[:], in_=k_phi_scale.rearrange("a c (p t) f -> p (a c t f)", t=PACK))
@@ -83,35 +83,36 @@ def tile_dpfpattention_pb_w4_kernel(tc, x, wv_words, wv_scales, beta, vo, k_phi_
         def load_weight():
             nc.sync.dma_start(out=ww[:], in_=wv_words.rearrange("g p n -> p g n"))
 
-        load_kphi(0,2,2)
-        load_kphi(0,6,2)
-        load_kphi(0,8,2)
         load_kphi(0,0,2)
-        load_kphi(0,4,2)
-        load_x(0,2,2)
+        load_kphi(0,6,2)
+        load_kphi(0,2,2)
         load_x(0,0,2)
-        load_weight()
+        load_kphi(0,4,2)
+        load_kphi(0,12,2)
+        load_x(0,2,2)
         load_weight_scales()
+        load_kphi(0,8,2)
+        load_kphi(0,14,2)
+        load_weight()
         load_kphi(0,10,2)
         load_vo(0,0)
-        load_kphi(1,4,4)
-        load_vo(0,1)
-        load_kphi(0,12,4)
-        load_x(1,0,4)
         load_kphi(1,0,4)
-        load_vo(1,0)
-        load_vo(1,1)
-        load_kphi(1,8,4)
-        load_W(1)
+        load_vo(0,1)
+        load_x(1,0,4)
+        load_kphi(1,4,4)
         load_W(0)
+        load_vo(1,0)
+        load_kphi(1,8,4)
         load_kphi(1,12,4)
+        load_vo(1,1)
+        load_W(1)
 
         beta_t = keep.tile([P, B * H, PACK, RUN], BF16, align_bytes=64, name="beta_t")
 
         betas = []
 
         def turn_beta():
-            bt = psum.tile([P, 2, P], F32, name="turn", bufs=3)
+            bt = psum.tile([P, 2, P], F32, name="turn", bufs=2)
             words = beta_rows[:].bitcast(F32)
             for u in range(2):
                 nc.tensor.transpose(bt[:, u, :], words[:, u : 2 * P : 2], ident[:])
@@ -128,7 +129,7 @@ def tile_dpfpattention_pb_w4_kernel(tc, x, wv_words, wv_scales, beta, vo, k_phi_
         xp, xg, xc = {}, {}, {}
 
         def turn_x(b, t):
-            ps = psum.tile([P, 2, 2, P], F32, name="turn", bufs=3)
+            ps = psum.tile([P, 2, 2, P], F32, name="turn", bufs=2)
             words = xs[b, t].bitcast(F32)
             for g in range(2):
                 for u in range(2):
@@ -192,7 +193,7 @@ def tile_dpfpattention_pb_w4_kernel(tc, x, wv_words, wv_scales, beta, vo, k_phi_
         vps, t1s, dvg, dvc = {}, {}, {}, {}
 
         def values(b, u, t):
-            ps = psum.tile([P, 512], F32, name="v", bufs=3)
+            ps = psum.tile([P, 512], F32, name="v", bufs=4)
             codes, scales = xc[b, t]
             for g in range(2):
                 nc.tensor.matmul_mx(
@@ -218,9 +219,11 @@ def tile_dpfpattention_pb_w4_kernel(tc, x, wv_words, wv_scales, beta, vo, k_phi_
             )
 
         def scale_dv(b, u, j):
-            dg = work.tile([P, 4, DH, PACK], BF16, align_bytes=64, name="dvg", bufs=3)
+            name = "dvg_last" if (b, u, j) == (1, 1, 1) else "dvg"
+            dg = work.tile([P, 4, DH, PACK], BF16, align_bytes=64, name="dvg", tag=name, bufs=1)
+            engine = nc.gpsimd if j == 1 and (b, u) != (1, 1) else nc.vector
             r0 = 16 * b + 8 * u + 4 * j
-            nc.vector.tensor_tensor(
+            engine.tensor_tensor(
                 out=dg[:].rearrange("p h (c i) t -> p h c t i", i=RUN),
                 in0=t1s[b, u][:, 4 * j : 4 * j + 4, :, :, :],
                 in1=beta_t[:, r0 : r0 + 4, :, :].unsqueeze(2).to_broadcast([P, 4, DH // RUN, PACK, RUN]),
@@ -263,141 +266,141 @@ def tile_dpfpattention_pb_w4_kernel(tc, x, wv_words, wv_scales, beta, vo, k_phi_
             nc.sync.dma_start(out=out[b, h0 : h0 + 4].rearrange("h s d -> s h d"), in_=ot[:])
 
         with tc.manual_schedule():
-            widen(0, 2)
-            widen(0, 6)
-            widen(0, 8)
-            interleave(0, 6)
             widen(0, 0)
-            interleave(0, 2)
-            turn_beta()
-            widen(0, 4)
-            turn_x(0, 3)
-            quant_k(0, 6)
-            interleave(0, 4)
-            interleave(0, 8)
-            turn_x(0, 2)
-            quant_k(0, 2)
-            quant_k(0, 4)
-            copy_x(0, 3)
+            widen(0, 6)
+            widen(0, 2)
             interleave(0, 0)
-            copy_x(0, 2)
-            turn_x(0, 1)
-            quant_k(0, 8)
+            widen(0, 4)
+            interleave(0, 2)
             quant_k(0, 0)
-            copy_beta()
             turn_x(0, 0)
-            quant_x(0, 2)
-            copy_x(0, 1)
-            quant_x(0, 3)
-            quant_x(0, 1)
             copy_x(0, 0)
-            values(0, 0, 2)
-            widen(0, 10)
-            values(0, 0, 3)
-            quant_x(0, 0)
-            interleave(0, 10)
-            values(0, 0, 1)
-            subtract(0, 0, 1)
-            subtract(0, 0, 3)
-            values(0, 0, 0)
-            widen(1, 4)
-            subtract(0, 0, 2)
-            values(0, 1, 3)
-            subtract(0, 0, 0)
-            values(0, 1, 2)
-            quant_k(0, 10)
-            widen(1, 6)
-            scale_dv(0, 0, 1)
-            values(0, 1, 0)
-            interleave(1, 4)
-            scale_dv(0, 0, 0)
-            subtract(0, 1, 2)
-            interleave(1, 6)
-            quant_dv(0, 0, 0)
-            values(0, 1, 1)
-            subtract(0, 1, 3)
-            widen(0, 14)
-            update(0, 0, 0)
-            quant_k(1, 6)
-            subtract(0, 1, 1)
-            turn_x(1, 0)
-            quant_dv(0, 0, 1)
+            turn_x(0, 1)
+            interleave(0, 6)
+            copy_x(0, 1)
             widen(0, 12)
-            subtract(0, 1, 0)
-            turn_x(1, 1)
-            quant_k(1, 4)
-            turn_x(1, 2)
-            scale_dv(0, 1, 1)
-            copy_x(1, 0)
-            update(0, 0, 1)
-            copy_x(1, 1)
-            turn_x(1, 3)
-            quant_x(1, 0)
-            quant_dv(0, 1, 1)
-            copy_x(1, 2)
-            values(1, 1, 0)
-            quant_x(1, 1)
-            copy_x(1, 3)
-            scale_dv(0, 1, 0)
-            values(1, 1, 1)
-            widen(1, 0)
-            values(1, 0, 1)
-            quant_x(1, 2)
-            quant_dv(0, 1, 0)
-            subtract(1, 1, 0)
+            interleave(0, 4)
+            quant_k(0, 2)
+            quant_x(0, 0)
+            quant_x(0, 1)
+            turn_x(0, 2)
+            copy_x(0, 2)
+            turn_x(0, 3)
+            copy_x(0, 3)
+            quant_k(0, 4)
+            widen(0, 8)
+            quant_x(0, 2)
+            quant_x(0, 3)
+            turn_beta()
+            copy_beta()
+            widen(0, 14)
             interleave(0, 12)
-            interleave(1, 0)
-            values(1, 0, 2)
-            quant_x(1, 3)
-            widen(1, 10)
-            subtract(1, 0, 1)
+            values(0, 0, 0)
+            values(0, 0, 1)
+            values(0, 0, 2)
+            values(0, 0, 3)
+            widen(0, 10)
+            interleave(0, 8)
+            quant_k(0, 6)
+            interleave(0, 10)
+            quant_k(0, 8)
+            subtract(0, 0, 0)
+            subtract(0, 0, 1)
+            subtract(0, 0, 2)
+            subtract(0, 0, 3)
+            values(0, 1, 0)
+            values(0, 1, 1)
+            values(0, 1, 2)
+            values(0, 1, 3)
+            quant_k(0, 10)
+            scale_dv(0, 0, 0)
             quant_k(0, 12)
-            values(1, 1, 3)
-            subtract(1, 1, 1)
-            widen(1, 8)
-            subtract(1, 0, 2)
-            values(1, 0, 3)
-            subtract(1, 1, 3)
-            values(1, 1, 2)
-            interleave(1, 10)
-            subtract(1, 0, 3)
-            values(1, 0, 0)
-            quant_k(1, 0)
-            subtract(1, 1, 2)
-            interleave(1, 8)
-            quant_k(1, 10)
-            finish(0, 0, 1)
-            finish(0, 0, 0)
-            update(0, 1, 0)
-            subtract(1, 0, 0)
-            widen(1, 2)
-            finish(0, 1, 0)
-            quant_k(1, 8)
-            scale_dv(1, 0, 0)
-            widen(1, 14)
-            scale_dv(1, 0, 1)
-            interleave(1, 2)
-            quant_dv(1, 0, 0)
-            scale_dv(1, 1, 1)
-            interleave(1, 14)
-            quant_k(1, 2)
-            quant_dv(1, 1, 1)
-            widen(1, 12)
-            update(1, 0, 0)
-            quant_dv(1, 0, 1)
-            scale_dv(1, 1, 0)
-            update(1, 0, 1)
+            quant_dv(0, 0, 0)
+            widen(1, 0)
             interleave(0, 14)
+            widen(1, 2)
+            interleave(1, 0)
+            turn_x(1, 0)
+            copy_x(1, 0)
+            turn_x(1, 1)
+            copy_x(1, 1)
+            update(0, 0, 0)
+            scale_dv(0, 0, 1)
+            subtract(0, 1, 0)
+            subtract(0, 1, 1)
+            subtract(0, 1, 2)
+            subtract(0, 1, 3)
+            quant_dv(0, 0, 1)
+            quant_k(0, 14)
+            turn_x(1, 2)
+            copy_x(1, 2)
+            turn_x(1, 3)
+            copy_x(1, 3)
+            interleave(1, 2)
+            update(0, 0, 1)
+            scale_dv(0, 1, 0)
+            quant_x(1, 0)
+            quant_x(1, 1)
+            quant_x(1, 2)
+            quant_x(1, 3)
+            values(1, 0, 0)
+            values(1, 0, 1)
+            values(1, 0, 2)
+            values(1, 0, 3)
+            finish(0, 0, 0)
+            quant_dv(0, 1, 0)
+            update(0, 1, 0)
+            widen(1, 4)
+            widen(1, 6)
+            interleave(1, 4)
+            scale_dv(0, 1, 1)
+            subtract(1, 0, 0)
+            subtract(1, 0, 1)
+            subtract(1, 0, 2)
+            subtract(1, 0, 3)
+            values(1, 1, 0)
+            values(1, 1, 1)
+            values(1, 1, 2)
+            values(1, 1, 3)
+            finish(0, 0, 1)
+            finish(0, 1, 0)
+            widen(1, 8)
+            interleave(1, 6)
+            quant_dv(0, 1, 1)
+            quant_k(1, 0)
+            update(0, 1, 1)
+            quant_k(1, 2)
+            scale_dv(1, 0, 0)
+            quant_k(1, 4)
+            quant_dv(1, 0, 0)
+            update(1, 0, 0)
+            widen(1, 10)
+            interleave(1, 8)
+            widen(1, 12)
+            interleave(1, 10)
+            widen(1, 14)
+            interleave(1, 12)
+            interleave(1, 14)
+            scale_dv(1, 0, 1)
+            subtract(1, 1, 0)
+            subtract(1, 1, 1)
+            subtract(1, 1, 2)
+            subtract(1, 1, 3)
+            finish(0, 1, 1)
             finish(1, 0, 0)
+            quant_dv(1, 0, 1)
+            quant_k(1, 6)
+            update(1, 0, 1)
+            scale_dv(1, 1, 0)
+            quant_k(1, 8)
+            scale_dv(1, 1, 1)
             quant_dv(1, 1, 0)
             finish(1, 0, 1)
+            quant_k(1, 10)
             update(1, 1, 0)
-            interleave(1, 12)
-            quant_k(0, 14)
-            quant_k(1, 14)
-            update(0, 1, 1)
-            finish(1, 1, 0)
-            finish(0, 1, 1)
+            quant_dv(1, 1, 1)
             quant_k(1, 12)
+            finish(1, 1, 0)
+            quant_k(1, 14)
             update(1, 1, 1)
             finish(1, 1, 1)

from contextlib import ExitStack

import concourse.mybir as mybir
from concourse.masks import make_identity

F32 = mybir.dt.float32
BF16 = mybir.dt.bfloat16
I32 = mybir.dt.int32
U32 = mybir.dt.uint32
U8 = mybir.dt.uint8
FP8 = mybir.dt.float8_e4m3fn
E4M3X4 = mybir.dt.float8_e4m3fn_x4
E2M1X4 = mybir.dt.float4_e2m1fn_x4
ALU = mybir.AluOpType
ACT = mybir.ActivationFunctionType

B, N, D, H, DH = 2, 512, 1024, 16, 64
S = 2 * DH
P = 128
PACK = 4
RUN = 4
FLOPS = 2 * B * N * D * H * DH + 2 * B * H * N * S * DH

WIDEN_ON_VECTOR = ((0, 0), (0, 2), (0, 4), (0, 8), (0, 10))
INTERLEAVE_ON_VECTOR = ((0, 0), (0, 2), (0, 4), (0, 8), (0, 10))


def tile_dpfpattention_pb_w4_kernel(tc, x, wv_words, wv_scales, beta, vo, k_phi_bytes, k_phi_scale, W, out):
    nc = tc.nc
    with ExitStack() as ctx:
        keep = ctx.enter_context(tc.tile_pool(name="keep", bufs=1))
        work = ctx.enter_context(tc.tile_pool(name="work", bufs=4))
        psum = ctx.enter_context(tc.psum_pool(name="psum", bufs=2))

        ident = keep.tile([P, P], F32, name="ident")
        make_identity(nc, ident[:])
        warm = keep.tile([P, 1], F32, name="warm")
        nc.vector.memset(warm[:], 0.0)
        nc.scalar.activation(out=warm[:], in_=warm[:], func=ACT.Copy)
        wsc = keep.tile([P, 2, D], U8, align_bytes=64, name="wsc")
        nc.vector.memset(wsc[:].rearrange("p g n -> p (g n)").bitcast(I32), 0)
        beta_rows = keep.tile([P, N], BF16, align_bytes=64, name="beta_rows")
        nc.vector.memset(beta_rows[:], 0.0)
        nc.gpsimd.dma_start(out=beta_rows[0 : B * H, :], in_=beta.rearrange("b h n -> (b h) n"))
        kscale = keep.tile([P, PACK], F32, name="kscale")
        nc.sync.dma_start(out=kscale[:], in_=k_phi_scale.rearrange("a c (p t) f -> p (a c t f)", t=PACK))
        kb, xs, vos, ws = {}, {}, {}, {}

        def load_kphi(b, h0, nh):
            kbt = keep.tile([P, nh, PACK * S], U8, align_bytes=64, name=f"kb_{b}_{h0}")
            nc.sync.dma_start(out=kbt[:], in_=k_phi_bytes[b, h0 : h0 + nh].rearrange("h (p t) s -> p h (t s)", t=PACK))
            for h in range(nh):
                kb[b, h0 + h] = kbt[:, h, :]

        def load_x(b, t0, nt):
            xt = keep.tile([P, nt, D], BF16, align_bytes=64, name=f"x_{b}_{t0}")
            nc.sync.dma_start(out=xt[:], in_=x[b].rearrange("(p t) k -> p t k", t=PACK)[:, t0 : t0 + nt, :])
            for t in range(nt):
                xs[b, t0 + t] = xt[:, t, :]

        def load_vo(b, u):
            v = keep.tile([P, 8, PACK, DH], BF16, align_bytes=64, name=f"vo_{b}_{u}")
            nc.sync.dma_start(
                out=v[:].rearrange("p h t d -> p h (t d)"),
                in_=vo[b, 8 * u : 8 * u + 8].rearrange("h (p t) d -> p h (t d)", t=PACK),
            )
            vos[b, u] = v

        def load_W(b):
            w = keep.tile([P, H, DH], BF16, align_bytes=64, name=f"W_{b}")
            nc.sync.dma_start(out=w[:], in_=W[b].rearrange("h s d -> s h d"))
            ws[b] = w

        ww = keep.tile([P, 2, 2 * D], U8, align_bytes=64, name="ww")

        def load_weight_scales():
            for q in range(4):
                nc.sync.dma_start(
                    out=wsc[32 * q : 32 * q + 4, :, :].bitcast(I32),
                    in_=wv_scales[:, 4 * q : 4 * q + 4, :].rearrange("g q n -> q g n").bitcast(I32),
                )

        def load_weight():
            nc.sync.dma_start(out=ww[:], in_=wv_words.rearrange("g p n -> p g n"))

        load_kphi(0,0,2)
        load_kphi(0,6,2)
        load_kphi(0,2,2)
        load_x(0,0,2)
        load_kphi(0,4,2)
        load_kphi(0,12,2)
        load_x(0,2,2)
        load_weight_scales()
        load_kphi(0,8,2)
        load_kphi(0,14,2)
        load_weight()
        load_kphi(0,10,2)
        load_vo(0,0)
        load_kphi(1,0,4)
        load_vo(0,1)
        load_x(1,0,4)
        load_kphi(1,4,4)
        load_W(0)
        load_vo(1,0)
        load_kphi(1,8,4)
        load_kphi(1,12,4)
        load_vo(1,1)
        load_W(1)

        beta_t = keep.tile([P, B * H, PACK, RUN], BF16, align_bytes=64, name="beta_t")

        betas = []

        def turn_beta():
            bt = psum.tile([P, 2, P], F32, name="turn", bufs=2)
            words = beta_rows[:].bitcast(F32)
            for u in range(2):
                nc.tensor.transpose(bt[:, u, :], words[:, u : 2 * P : 2], ident[:])
            betas.append(bt)

        def copy_beta():
            for u in range(2):
                pair = betas[0][:, u, 0 : B * H].bitcast(BF16).rearrange("p (r e) -> p r e", e=2)
                nc.scalar.copy(
                    out=beta_t[:, :, 2 * u : 2 * u + 2, :],
                    in_=pair.unsqueeze(3).to_broadcast([P, B * H, 2, RUN]),
                )

        xp, xg, xc = {}, {}, {}

        def turn_x(b, t):
            ps = psum.tile([P, 2, 2, P], F32, name="turn", bufs=2)
            words = xs[b, t].bitcast(F32)
            for g in range(2):
                for u in range(2):
                    nc.tensor.transpose(ps[:, g, u, :], words[:, 256 * g + u : 256 * (g + 1) : 2], ident[:])
            xp[b, t] = ps

        def copy_x(b, t):
            ps = xp[b, t]
            gt = work.tile([P, 2 * P * PACK], BF16, align_bytes=64, name="xg", bufs=8)
            nc.scalar.copy(
                out=gt[:].bitcast(F32).rearrange("p (g r u) -> p g r u", g=2, u=2),
                in_=ps[:].rearrange("p g u r -> p g r u"),
            )
            xg[b, t] = gt

        def quant_x(b, t):
            codes = keep.tile([P, 2, P], U32, align_bytes=64, name=f"xc_{b}_{t}")
            scales = keep.tile([P, 2, P], U8, align_bytes=64, name=f"xsc_{b}_{t}")
            nc.vector.quantize_mx(
                out=codes[:].rearrange("p g r -> p (g r)").bitcast(E4M3X4),
                scales=scales[:].rearrange("p g r -> p (g r)"),
                in_=xg[b, t][:],
            )
            xc[b, t] = (codes, scales)

        planes, inter, kc = {}, {}, {}

        def widen(b, h):
            pl = work.tile([P, 2, PACK, S], BF16, align_bytes=64, name="planes", bufs=16)
            for i in range(2):
                for t in range(PACK):
                    src = kb[b, h + i][:, S * t : S * (t + 1)].bitcast(FP8)
                    if (b, h) in WIDEN_ON_VECTOR:
                        nc.vector.tensor_scalar(out=pl[:, i, t, :], in0=src, scalar1=kscale[:, t : t + 1], scalar2=None, op0=ALU.mult)
                    else:
                        nc.scalar.activation(out=pl[:, i, t, :], in_=src, func=ACT.Copy, scale=kscale[:, t : t + 1])
            planes[b, h] = pl

        def interleave(b, h):
            pl = planes[b, h]
            it = work.tile([P, 2, S, PACK], BF16, align_bytes=64, name="inter", bufs=16)
            copy = nc.vector.tensor_copy if (b, h) in INTERLEAVE_ON_VECTOR else nc.scalar.copy
            for i in range(2):
                copy(
                    out=it[:, i, :, :].rearrange("p (c i) t -> p c t i", i=RUN),
                    in_=pl[:, i, :, :].rearrange("p t (c i) -> p c t i", i=RUN),
                )
            inter[b, h] = it

        def quant_k(b, h):
            codes = keep.tile([P, 2, S], U32, align_bytes=64, name=f"kc_{b}_{h}")
            scales = keep.tile([P, 2, S], U8, align_bytes=64, name=f"ksc_{b}_{h}")
            nc.vector.quantize_mx(
                out=codes[:].rearrange("p h s -> p (h s)").bitcast(E4M3X4),
                scales=scales[:].rearrange("p h s -> p (h s)"),
                in_=inter[b, h][:].rearrange("p h s t -> p (h s t)"),
            )
            for i in range(2):
                kc[b, h + i] = (codes[:, i, :], scales[:, i, :])

        vps, t1s, dvg, dvc = {}, {}, {}, {}

        def values(b, u, t):
            ps = psum.tile([P, 512], F32, name="v", bufs=4)
            codes, scales = xc[b, t]
            for g in range(2):
                nc.tensor.matmul_mx(
                    out=ps[:],
                    lhsT=codes[:, g, :].bitcast(E4M3X4),
                    lhsT_scale=scales[:, g, :],
                    rhs=ww[:, g, 1024 * u : 1024 * (u + 1)].bitcast(E2M1X4),
                    rhs_scale=wsc[:, g, 512 * u : 512 * (u + 1)],
                    start=(g == 0),
                    stop=(g == 1),
                )
            vps[b, u, t] = ps

        def subtract(b, u, t):
            if (b, u) not in t1s:
                t1 = work.tile([P, 8, DH // RUN, PACK, RUN], F32, align_bytes=64, name="t1", bufs=3)
                t1s[b, u] = t1
            nc.vector.tensor_tensor(
                out=t1s[b, u][:, :, :, t, :],
                in0=vps[b, u, t][:].rearrange("p (h c i) -> p h c i", h=8, i=RUN),
                in1=vos[b, u][:, :, t, :].rearrange("p h (c i) -> p h c i", i=RUN),
                op=ALU.subtract,
            )

        def scale_dv(b, u, j):
            name = "dvg_last" if (b, u, j) == (1, 1, 1) else "dvg"
            dg = work.tile([P, 4, DH, PACK], BF16, align_bytes=64, name="dvg", tag=name, bufs=1)
            engine = nc.gpsimd if j == 1 and (b, u) != (1, 1) else nc.vector
            r0 = 16 * b + 8 * u + 4 * j
            engine.tensor_tensor(
                out=dg[:].rearrange("p h (c i) t -> p h c t i", i=RUN),
                in0=t1s[b, u][:, 4 * j : 4 * j + 4, :, :, :],
                in1=beta_t[:, r0 : r0 + 4, :, :].unsqueeze(2).to_broadcast([P, 4, DH // RUN, PACK, RUN]),
                op=ALU.mult,
            )
            dvg[b, u, j] = dg

        def quant_dv(b, u, j):
            codes = work.tile([P, 4, DH], U32, align_bytes=64, name="dvc", bufs=4)
            scales = work.tile([P, 4, DH], U8, align_bytes=64, name="dvsc", bufs=4)
            nc.vector.quantize_mx(
                out=codes[:].rearrange("p h d -> p (h d)").bitcast(E4M3X4),
                scales=scales[:].rearrange("p h d -> p (h d)"),
                in_=dvg[b, u, j][:].rearrange("p h d t -> p (h d t)"),
            )
            dvc[b, u, j] = (codes, scales)

        ops = {}

        def update(b, u, j):
            ps = psum.tile([P, 4, DH], F32, name="o", bufs=2)
            dcodes, dscales = dvc[b, u, j]
            for i in range(4):
                kcodes, kscales = kc[b, 8 * u + 4 * j + i // 2 * 2 + i % 2]
                nc.tensor.matmul_mx(
                    out=ps[:, i, :],
                    lhsT=kcodes.bitcast(E4M3X4),
                    lhsT_scale=kscales,
                    rhs=dcodes[:, i, :].bitcast(E4M3X4),
                    rhs_scale=dscales[:, i, :],
                    start=True,
                    stop=True,
                )
            ops[b, u, j] = ps

        def finish(b, u, j):
            h0 = 8 * u + 4 * j
            ot = work.tile([P, 4, DH], F32, align_bytes=64, name="ot", bufs=4)
            nc.vector.tensor_tensor(out=ot[:], in0=ops[b, u, j][:], in1=ws[b][:, h0 : h0 + 4, :], op=ALU.add)
            nc.sync.dma_start(out=out[b, h0 : h0 + 4].rearrange("h s d -> s h d"), in_=ot[:])

        with tc.manual_schedule():
            widen(0, 0)
            widen(0, 6)
            widen(0, 2)
            interleave(0, 0)
            widen(0, 4)
            interleave(0, 2)
            quant_k(0, 0)
            turn_x(0, 0)
            copy_x(0, 0)
            turn_x(0, 1)
            interleave(0, 6)
            copy_x(0, 1)
            widen(0, 12)
            interleave(0, 4)
            quant_k(0, 2)
            quant_x(0, 0)
            quant_x(0, 1)
            turn_x(0, 2)
            copy_x(0, 2)
            turn_x(0, 3)
            copy_x(0, 3)
            quant_k(0, 4)
            widen(0, 8)
            quant_x(0, 2)
            quant_x(0, 3)
            turn_beta()
            copy_beta()
            widen(0, 14)
            interleave(0, 12)
            values(0, 0, 0)
            values(0, 0, 1)
            values(0, 0, 2)
            values(0, 0, 3)
            widen(0, 10)
            interleave(0, 8)
            quant_k(0, 6)
            interleave(0, 10)
            quant_k(0, 8)
            subtract(0, 0, 0)
            subtract(0, 0, 1)
            subtract(0, 0, 2)
            subtract(0, 0, 3)
            values(0, 1, 0)
            values(0, 1, 1)
            values(0, 1, 2)
            values(0, 1, 3)
            quant_k(0, 10)
            scale_dv(0, 0, 0)
            quant_k(0, 12)
            quant_dv(0, 0, 0)
            widen(1, 0)
            interleave(0, 14)
            widen(1, 2)
            interleave(1, 0)
            turn_x(1, 0)
            copy_x(1, 0)
            turn_x(1, 1)
            copy_x(1, 1)
            update(0, 0, 0)
            scale_dv(0, 0, 1)
            subtract(0, 1, 0)
            subtract(0, 1, 1)
            subtract(0, 1, 2)
            subtract(0, 1, 3)
            quant_dv(0, 0, 1)
            quant_k(0, 14)
            turn_x(1, 2)
            copy_x(1, 2)
            turn_x(1, 3)
            copy_x(1, 3)
            interleave(1, 2)
            update(0, 0, 1)
            scale_dv(0, 1, 0)
            quant_x(1, 0)
            quant_x(1, 1)
            quant_x(1, 2)
            quant_x(1, 3)
            values(1, 0, 0)
            values(1, 0, 1)
            values(1, 0, 2)
            values(1, 0, 3)
            finish(0, 0, 0)
            quant_dv(0, 1, 0)
            update(0, 1, 0)
            widen(1, 4)
            widen(1, 6)
            interleave(1, 4)
            scale_dv(0, 1, 1)
            subtract(1, 0, 0)
            subtract(1, 0, 1)
            subtract(1, 0, 2)
            subtract(1, 0, 3)
            values(1, 1, 0)
            values(1, 1, 1)
            values(1, 1, 2)
            values(1, 1, 3)
            finish(0, 0, 1)
            finish(0, 1, 0)
            widen(1, 8)
            interleave(1, 6)
            quant_dv(0, 1, 1)
            quant_k(1, 0)
            update(0, 1, 1)
            quant_k(1, 2)
            scale_dv(1, 0, 0)
            quant_k(1, 4)
            quant_dv(1, 0, 0)
            update(1, 0, 0)
            widen(1, 10)
            interleave(1, 8)
            widen(1, 12)
            interleave(1, 10)
            widen(1, 14)
            interleave(1, 12)
            interleave(1, 14)
            scale_dv(1, 0, 1)
            subtract(1, 1, 0)
            subtract(1, 1, 1)
            subtract(1, 1, 2)
            subtract(1, 1, 3)
            finish(0, 1, 1)
            finish(1, 0, 0)
            quant_dv(1, 0, 1)
            quant_k(1, 6)
            update(1, 0, 1)
            scale_dv(1, 1, 0)
            quant_k(1, 8)
            scale_dv(1, 1, 1)
            quant_dv(1, 1, 0)
            finish(1, 0, 1)
            quant_k(1, 10)
            update(1, 1, 0)
            quant_dv(1, 1, 1)
            quant_k(1, 12)
            finish(1, 1, 0)
            quant_k(1, 14)
            update(1, 1, 1)
            finish(1, 1, 1)
